import numpy as np
import ml_dtypes


def mxq(x, axis, fmt="e4m3"):
    dtype, down = {"e4m3": (ml_dtypes.float8_e4m3fn, 7), "e5m2": (ml_dtypes.float8_e5m2, 14)}[fmt]
    v = np.moveaxis(np.asarray(x, np.float32).astype(ml_dtypes.bfloat16).astype(np.float64), axis, -1)
    blocks = v.reshape(v.shape[:-1] + (-1, 32))
    amax = np.abs(blocks).max(-1, keepdims=True)
    byte = np.maximum(np.where(amax > 0, np.frexp(amax)[1] - 1 + 127, 0) - down, 1)
    scale = np.exp2(byte - 127.0)
    codes = (blocks / scale).astype(np.float32).astype(dtype).astype(np.float64)
    return np.moveaxis((codes * scale).reshape(v.shape), -1, axis)


WIDE = False


def mx_kscale(k):
    if not WIDE:
        return np.ones(k)
    levels = np.array([10, -10, 5, -5, 0])
    if k % 512:
        return np.exp2(np.random.permutation(np.resize(levels, k // 32))).repeat(32)
    a = np.empty((k // 512, 16))
    for p in range(k // 512):
        a[p, :8] = np.random.permutation(np.resize(levels, 8))
        for g in range(8):
            far = levels[np.abs(levels - a[p, g]) >= 10]
            a[p, g + 8] = far[np.random.randint(len(far))]
    return np.exp2(a.ravel()).repeat(32)


BF16 = ml_dtypes.bfloat16


def bf(x):
    return np.asarray(x, np.float32).astype(BF16)


def f64(x):
    return np.asarray(x).astype(np.float64)


B, O, D, G1, G2, F1, F2 = 256, 8, 1024, 1024, 1024, 1024, 1024
C = D + D
P = O * O


def setup_inputs():
    s = mx_kscale(C)[:D]
    ss = np.concatenate([s, s])
    t = mx_kscale(G1)
    return {
        "objs": bf(np.random.standard_normal((B, O, D)) * s),
        "W1": bf(np.random.standard_normal((G1, C)) / np.sqrt(C) / ss * t[:, None]),
        "b1": bf(np.random.standard_normal(G1) * 0.3 * t),
        "W2": bf(np.random.standard_normal((G2, G1)) * 0.5 / np.sqrt(G1) / t),
        "b2": bf(np.random.standard_normal(G2) * 0.15),
    }


def reference(objs, W1, b1, W2, b2):
    v = f64(objs)
    v_i = np.broadcast_to(v[:, None, :, :], (B, O, O, D))
    v_j = np.broadcast_to(v[:, :, None, :], (B, O, O, D))
    pairs = np.concatenate([v_i, v_j], axis=-1).reshape(B, P, C)
    h = np.maximum((mxq(pairs, 2, "e4m3") @ mxq(f64(W1).T, 0, "e4m3")) + f64(b1), 0.0)
    x_pairs = np.maximum((mxq(h, 2, "e4m3") @ mxq(f64(W2).T, 0, "e4m3")) + f64(b2), 0.0)
    return x_pairs, x_pairs.sum(axis=1)

@@ -1,0 +1,381 @@
+from contextlib import ExitStack
+
+import concourse.mybir as mybir
+from concourse.masks import make_identity
+
+F32 = mybir.dt.float32
+BF16 = mybir.dt.bfloat16
+U32 = mybir.dt.uint32
+U8 = mybir.dt.uint8
+FP8X4 = mybir.dt.float8_e4m3fn_x4
+RELU = mybir.ActivationFunctionType.Relu
+ADD = mybir.AluOpType.add
+
+SETS, OBJ, FEAT, HID, OUTC = 256, 8, 1024, 1024, 1024
+PAIRS = OBJ * OBJ
+FLOPS = 2 * SETS * PAIRS * (2 * FEAT * HID + HID * OUTC)
+
+P = 128
+UNIT_SETS = 8
+UNITS = SETS // UNIT_SETS
+CHUNKS = SETS * OBJ // P
+BANKS = {"y": 3, "xo": 4, "s1": 1}
+
+
+def tile_pairwiserelationmodule_pa_l_kernel(tc, objs, W1, b1, W2, b2, out_0, out_1):
+    nc = tc.nc
+    objs_rows = objs.flatten_outer_dims()
+    x_rows = out_0.flatten_outer_dims()
+
+    with ExitStack() as ctx:
+        ctx.enter_context(tc.manual_schedule())
+        keep = ctx.enter_context(tc.tile_pool(name="keep", bufs=1))
+        ring = ctx.enter_context(tc.tile_pool(name="ring", bufs=2))
+        psum = ctx.enter_context(tc.psum_pool(name="psum", bufs=2))
+
+        def bank(tag):
+            return psum.tile([P, 512], F32, name="bank_" + tag, tag=tag, bufs=BANKS[tag])
+
+        ident = keep.tile([P, P], F32, name="ident")
+        make_identity(nc, ident[:])
+        b1_bf = keep.tile([P, 2, 4], BF16, name="b1_bf")
+        b2_bf = keep.tile([P, 8], BF16, name="b2_bf")
+        b1_f = keep.tile([P, 2, 4], F32, name="b1_f")
+        b2_f = keep.tile([P, 8], F32, name="b2_f")
+        warm = keep.tile([P, 1], F32, name="warm")
+        w1_codes = keep.tile([P, 4, HID], U32, name="w1_codes", align_bytes=64)
+        w1_scales = keep.tile([P, 4, HID], U8, name="w1_scales", align_bytes=64)
+        w2_codes = keep.tile([P, 2, OUTC], U32, name="w2_codes", align_bytes=64)
+        w2_scales = keep.tile([P, 2, OUTC], U8, name="w2_scales", align_bytes=64)
+        s_t = [keep.tile([P, 8, P], F32, name="s_t%d" % h) for h in range(2)]
+        obj_raw = [keep.tile([P, 2, FEAT], BF16, name="obj_raw%d" % r) for r in range(8)]
+
+        with nc.allow_non_contiguous_dma(reason="two small bias vectors, one or four elements a partition"):
+            nc.scalar.dma_start(out=b1_bf[:], in_=b1.rearrange("(g p t) -> p g t", g=2, t=4))
+            nc.scalar.dma_start(out=b2_bf[:], in_=b2.rearrange("(j p) -> p j", p=P))
+        nc.vector.memset(warm[:], 0.0)
+        nc.scalar.activation(out=warm[:], in_=warm[:], func=RELU)
+
+        def load_objs(r):
+            nc.sync.dma_start(
+                out=obj_raw[r][:],
+                in_=objs_rows[256 * r : 256 * (r + 1), :].rearrange("(i p) k -> p i k", p=P),
+            )
+
+        def copy_out(engine, out, in_):
+            if engine == "v":
+                nc.vector.tensor_copy(out=out, in_=in_)
+            else:
+                nc.scalar.copy(out=out, in_=in_)
+
+        def turn_two(tag, rows_a, rows_b):
+            bk = bank(tag)
+            view = bk[:].rearrange("p (s u r) -> p s u r", s=2, u=2)
+            for s, rows in enumerate((rows_a, rows_b)):
+                words = rows.bitcast(F32)
+                for u in range(2):
+                    nc.tensor.transpose(view[:, s, u, :], words[:, u : 256 : 2], ident[:])
+            return view.rearrange("p s u r -> p s r u")
+
+        def group_two(engine, turned, grouped_words):
+            copy_out(engine, grouped_words.rearrange("p (s r u) -> p s r u", s=2, u=2), turned)
+
+        obj_q = {}
+        ab = {}
+
+        def objs_turn(c, tag):
+            rows = obj_raw[c // 2][:, c % 2, :]
+            obj_q[c] = [
+                turn_two(tag, rows[:, 0:512], rows[:, 512:1024]),
+                ring.tile([P, 1024], BF16, name="obj_grouped", bufs=2, align_bytes=64),
+                ring.tile([P, 2, P], U32, name="obj_code", bufs=4, align_bytes=64),
+                ring.tile([P, 2, P], U8, name="obj_scale", bufs=4, align_bytes=64),
+            ]
+
+        def objs_group(c, engine):
+            group_two(engine, obj_q[c][0], obj_q[c][1][:].bitcast(F32))
+
+        def objs_quant(c):
+            nc.vector.quantize_mx(
+                out=obj_q[c][2][:].rearrange("p c o -> p (c o)").bitcast(FP8X4),
+                scales=obj_q[c][3][:].rearrange("p c o -> p (c o)"),
+                in_=obj_q[c][1][:],
+            )
+
+        def stage1(c, half, g, tag):
+            if c not in ab:
+                ab[c] = [
+                    ring.tile([P, 2, P, 4], F32, name="a_sum", bufs=3),
+                    ring.tile([P, 2, P, 4], F32, name="b_sum", bufs=3),
+                ]
+            codes, scales = obj_q[c][2], obj_q[c][3]
+            bk = bank(tag)
+            view = bk[:].rearrange("p (t o) -> p t o", t=4)
+            for t in range(4):
+                cols = slice(512 * g + P * t, 512 * g + P * (t + 1))
+                for c2 in range(2):
+                    nc.tensor.matmul_mx(
+                        out=view[:, t, :],
+                        lhsT=w1_codes[:, 2 * half + c2, cols].bitcast(FP8X4),
+                        lhsT_scale=w1_scales[:, 2 * half + c2, cols],
+                        rhs=codes[:, c2, :].bitcast(FP8X4),
+                        rhs_scale=scales[:, c2, :],
+                        start=(c2 == 0),
+                        stop=(c2 == 1),
+                    )
+            return (c, half, g, view.rearrange("p t o -> p o t"))
+
+        def stage1_out(engine, c, half, g, sums):
+            if half == 0:
+                copy_out(engine, ab[c][0][:, g, :, :], sums)
+            else:
+                nc.vector.tensor_tensor(
+                    out=ab[c][1][:, g, :, :],
+                    in0=sums,
+                    in1=b1_f[:, g, :].unsqueeze(1).to_broadcast([P, P, 4]),
+                    op=ADD,
+                )
+
+        hid = {}
+
+        def h_add(u, g):
+            if u not in hid:
+                hid[u] = [
+                    ring.tile([P, 2, 2048], BF16, name="h_sum", bufs=2, align_bytes=64),
+                    ring.tile([P, 2, 2048], BF16, name="h_relu", bufs=2, align_bytes=64),
+                    ring.tile([P, 2, 512], U32, name="h_code", bufs=3, align_bytes=64),
+                    ring.tile([P, 2, 512], U8, name="h_scale", bufs=3, align_bytes=64),
+                ]
+            c, hf = divmod(u, 2)
+            o = slice(64 * hf, 64 * hf + 64)
+            shape = [P, UNIT_SETS, OBJ, OBJ, 4]
+            nc.vector.tensor_tensor(
+                out=hid[u][0][:, g, :].rearrange("p (b k m t) -> p b k m t", b=UNIT_SETS, k=OBJ, m=OBJ),
+                in0=ab[c][0][:, g, o, :].rearrange("p (b m) t -> p b m t", m=OBJ).unsqueeze(2).to_broadcast(shape),
+                in1=ab[c][1][:, g, o, :].rearrange("p (b k) t -> p b k t", k=OBJ).unsqueeze(3).to_broadcast(shape),
+                op=ADD,
+            )
+
+        def h_relu(u, g):
+            nc.vector.tensor_scalar_max(out=hid[u][1][:, g, :], in0=hid[u][0][:, g, :], scalar1=0.0)
+
+        def h_quant(u, g):
+            nc.vector.quantize_mx(
+                out=hid[u][2][:, g, :].bitcast(FP8X4), scales=hid[u][3][:, g, :], in_=hid[u][1][:, g, :]
+            )
+
+        pools = {}
+
+        def w2_quant(g, jq, grouped):
+            nc.vector.quantize_mx(
+                out=w2_codes[:, g, 512 * jq : 512 * (jq + 1)].bitcast(FP8X4),
+                scales=w2_scales[:, g, 512 * jq : 512 * (jq + 1)],
+                in_=grouped[:],
+            )
+
+        y_bank = {}
+        x_t = {}
+        x_bank = {}
+        x_sb = {}
+
+        def stage2(u, j):
+            y_bank[u, j] = bank("y")
+            for g in range(2):
+                nc.tensor.matmul_mx(
+                    out=y_bank[u, j][:],
+                    lhsT=w2_codes[:, g, P * j : P * (j + 1)].bitcast(FP8X4),
+                    lhsT_scale=w2_scales[:, g, P * j : P * (j + 1)],
+                    rhs=hid[u][2][:, g, :].bitcast(FP8X4),
+                    rhs_scale=hid[u][3][:, g, :],
+                    start=(g == 0),
+                    stop=(g == 1),
+                )
+
+        def stage2_out(u, j):
+            x_t[u, j] = pools["flow"].tile([P, 512], F32, name="x_t", bufs=16)
+            for bl in range(UNIT_SETS):
+                b = UNIT_SETS * u + bl
+                nc.scalar.activation(
+                    out=x_t[u, j][:, PAIRS * bl : PAIRS * (bl + 1)],
+                    in_=y_bank[u, j][:, PAIRS * bl : PAIRS * (bl + 1)],
+                    func=RELU,
+                    bias=b2_f[:, j : j + 1],
+                    scale=1.0,
+                    accum_out=s_t[b // P][:, j, b % P : b % P + 1],
+                )
+
+        def turn_x(u, tt):
+            x_sb[u, tt] = pools["flow"].tile([P, OUTC], F32, name="x_sb", bufs=6)
+            for hh in range(2):
+                x_bank[u, tt, hh] = bank("xo")
+                for jj in range(4):
+                    nc.tensor.transpose(
+                        x_bank[u, tt, hh][:, P * jj : P * (jj + 1)],
+                        x_t[u, 4 * hh + jj][:, P * tt : P * (tt + 1)],
+                        ident[:],
+                    )
+
+        def x_out(engine, u, tt, hh):
+            copy_out(engine, x_sb[u, tt][:, 512 * hh : 512 * (hh + 1)], x_bank[u, tt, hh][:])
+
+        def x_store(u, tt):
+            r0 = 512 * u + P * tt
+            nc.sync.dma_start(out=x_rows[r0 : r0 + P, :], in_=x_sb[u, tt][:])
+
+        s_sb = {}
+
+        def s_turn(h, hh):
+            if hh == 0:
+                s_sb[h] = pools["flow"].tile([P, OUTC], F32, name="x_sb", bufs=6)
+            bk = bank("s1")
+            for jj in range(4):
+                nc.tensor.transpose(bk[:, P * jj : P * (jj + 1)], s_t[h][:, 4 * hh + jj, :], ident[:])
+            return bk
+
+        def s_out(engine, h, hh, bk):
+            copy_out(engine, s_sb[h][:, 512 * hh : 512 * (hh + 1)], bk[:])
+            if hh == 1:
+                nc.sync.dma_start(out=out_1[P * h : P * (h + 1), :], in_=s_sb[h][:])
+
+        S_SLOT = {2 * UNITS - 6: (0, 0), 2 * UNITS - 5: (0, 1), 2 * UNITS: (1, 0), 2 * UNITS + 1: (1, 1)}
+
+        def run_slot(slot, early, late_w2):
+            u, i = divmod(slot, 2)
+            js = list(range(4 * i, 4 * i + 4))
+            tts = (2 * i, 2 * i + 1)
+            add_u, add_g = divmod(slot + 3, 2)
+            fin_u, fin_g = divmod(slot + 2, 2)
+            c1, r1 = divmod(slot + 7, 4)
+            c0 = (slot + 9) // 4 if (slot + 9) % 4 == 0 else CHUNKS
+            if 0 <= u < UNITS:
+                for j in js[:3]:
+                    stage2(u, j)
+                stage2_out(u, js[0])
+                stage2(u, js[3])
+            if slot < 1:
+                sums = early[2 * slot + 2 : 2 * slot + 4]
+            else:
+                sums = [stage1(c1, r1 % 2, r1 // 2, "s1")] if c1 < CHUNKS else []
+            pu, pi = divmod(slot - 1, 2)
+            ptts = (2 * pi, 2 * pi + 1)
+            if 1 <= pu <= UNITS:
+                x_out("v", pu - 1, ptts[0], 0)
+                x_store(pu - 1, ptts[0])
+            if fin_u < UNITS:
+                h_relu(fin_u, fin_g)
+            if 1 <= pu <= UNITS:
+                x_out("v", pu - 1, ptts[1], 0)
+                x_store(pu - 1, ptts[1])
+            if fin_u < UNITS:
+                h_quant(fin_u, fin_g)
+            for g, jq, grouped in late_w2:
+                w2_quant(g, jq, grouped)
+            if 1 <= u <= UNITS:
+                for tt in tts:
+                    turn_x(u - 1, tt)
+            if 0 <= u < UNITS:
+                for j in js[1:]:
+                    stage2_out(u, j)
+            for done in sums:
+                if done[1] == 0:
+                    stage1_out("s", *done)
+            if add_u < UNITS:
+                h_add(add_u, add_g)
+            for done in sums:
+                if done[1] == 1:
+                    stage1_out("v", *done)
+            if c0 < CHUNKS:
+                objs_turn(c0, "s1")
+            s_bank = s_turn(*S_SLOT[slot]) if slot in S_SLOT else None
+            if 1 <= u <= UNITS:
+                for tt in tts:
+                    x_out("s", u - 1, tt, 1)
+            if c0 < CHUNKS:
+                objs_group(c0, "s")
+                objs_quant(c0)
+            if s_bank is not None:
+                s_out("v", S_SLOT[slot][0], S_SLOT[slot][1], s_bank)
+
+        load_objs(0)
+        with tc.tile_pool(name="prep", bufs=2) as prep:
+            w1_raw = {}
+            for g in range(2):
+                for q in range(4):
+                    w1_raw[g, q] = prep.tile([P, 4, 512], BF16, name="w1_raw", bufs=8)
+                    nc.sync.dma_start(
+                        out=w1_raw[g, q][:],
+                        in_=W1[512 * g : 512 * (g + 1), 512 * q : 512 * (q + 1)].rearrange("(m t) k -> m t k", t=4),
+                    )
+            w2_raw = {}
+            for g in range(2):
+                w2_raw[g] = prep.tile([P, 8, 512], BF16, name="w2_raw", bufs=2)
+                nc.sync.dma_start(
+                    out=w2_raw[g][:],
+                    in_=W2[:, 512 * g : 512 * (g + 1)].rearrange("(j p) k -> p j k", p=P),
+                )
+            for r in range(1, 8):
+                load_objs(r)
+
+            nc.vector.tensor_copy(out=b1_f[:], in_=b1_bf[:])
+            nc.vector.tensor_copy(out=b2_f[:], in_=b2_bf[:])
+
+            spare = ["xo", "y", "xo", "y", "xo", "y", "xo"]
+            count = [0]
+
+            def weights_turn(raw, slot0):
+                grouped = prep.tile([P, 2048], BF16, name="w_grouped", bufs=4, align_bytes=64)
+                words = grouped[:].bitcast(F32)
+                for d in (0, 2):
+                    tag = spare[count[0] % 7]
+                    count[0] += 1
+                    turned = turn_two(tag, raw[:, slot0 + d, :], raw[:, slot0 + d + 1, :])
+                    group_two("s", turned, words[:, 256 * d : 256 * d + 512])
+                return grouped
+
+            def w1_quant(g, q, grouped):
+                nc.vector.quantize_mx(
+                    out=w1_codes[:, q, 512 * g : 512 * (g + 1)].bitcast(FP8X4),
+                    scales=w1_scales[:, q, 512 * g : 512 * (g + 1)],
+                    in_=grouped[:],
+                )
+
+            objs_turn(0, "s1")
+            objs_turn(1, "y")
+            objs_group(0, "s")
+            objs_group(1, "s")
+            objs_quant(0)
+            objs_quant(1)
+            for q in range(4):
+                w1_quant(0, q, weights_turn(w1_raw[0, q], 0))
+            g10 = weights_turn(w1_raw[1, 0], 0)
+            sa = stage1(0, 0, 0, "s1")
+            sb = stage1(0, 1, 0, "y")
+            stage1_out("s", *sa)
+            stage1_out("v", *sb)
+            g11 = weights_turn(w1_raw[1, 1], 0)
+            h_add(0, 0)
+            w1_quant(1, 0, g10)
+            w1_quant(1, 1, g11)
+            g12 = weights_turn(w1_raw[1, 2], 0)
+            g13 = weights_turn(w1_raw[1, 3], 0)
+            h_relu(0, 0)
+            w1_quant(1, 2, g12)
+            w1_quant(1, 3, g13)
+            sa = stage1(0, 0, 1, "s1")
+            sb = stage1(0, 1, 1, "y")
+            stage1_out("s", *sa)
+            h_quant(0, 0)
+            stage1_out("v", *sb)
+            g20 = weights_turn(w2_raw[0], 0)
+            g22 = weights_turn(w2_raw[1], 0)
+            h_add(0, 1)
+            w2_quant(0, 0, g20)
+            w2_quant(1, 0, g22)
+            g21 = weights_turn(w2_raw[0], 4)
+            g23 = weights_turn(w2_raw[1], 4)
+            early = [stage1(1, r % 2, r // 2, "xo") for r in range(4)]
+            run_slot(-1, early, ((0, 1, g21), (1, 1, g23)))
+
+        pools["flow"] = ctx.enter_context(tc.tile_pool(name="flow", bufs=2))
+        for slot in range(2 * UNITS + 3):
+            run_slot(slot, early, ())

@@ -19,6 +19,8 @@ P = 128
 UNIT_SETS = 8
 UNITS = SETS // UNIT_SETS
 CHUNKS = SETS * OBJ // P
+S_BANK = (1, 1)
+G_SETS = 3
 BANKS = {"y": 3, "xo": 4, "s1": 1}
 
 
@@ -137,31 +139,37 @@ def tile_pairwiserelationmodule_pa_l_kernel(tc, objs, W1, b1, W2, b2, out_0, out
                 )
 
         hid = {}
+        h_code = {}
 
-        def h_add(u, g):
-            if u not in hid:
-                hid[u] = [
-                    ring.tile([P, 2, 2048], BF16, name="h_sum", bufs=2, align_bytes=64),
-                    ring.tile([P, 2, 2048], BF16, name="h_relu", bufs=2, align_bytes=64),
-                    ring.tile([P, 2, 512], U32, name="h_code", bufs=3, align_bytes=64),
-                    ring.tile([P, 2, 512], U8, name="h_scale", bufs=3, align_bytes=64),
-                ]
+        def h_add(engine, x, b0, b_end):
+            u, g = divmod(x, 2)
+            if x not in hid:
+                hid[x] = [ring.tile([P, 2048], BF16, name="h_sum", bufs=2, align_bytes=64)]
+            if b_end == b0:
+                return
             c, hf = divmod(u, 2)
-            o = slice(64 * hf, 64 * hf + 64)
-            shape = [P, UNIT_SETS, OBJ, OBJ, 4]
-            nc.vector.tensor_tensor(
-                out=hid[u][0][:, g, :].rearrange("p (b k m t) -> p b k m t", b=UNIT_SETS, k=OBJ, m=OBJ),
+            o = slice(64 * hf + OBJ * b0, 64 * hf + OBJ * b_end)
+            shape = [P, b_end - b0, OBJ, OBJ, 4]
+            engine.tensor_tensor(
+                out=hid[x][0][:, 256 * b0 : 256 * b_end].rearrange("p (b k m t) -> p b k m t", k=OBJ, m=OBJ, t=4),
                 in0=ab[c][0][:, g, o, :].rearrange("p (b m) t -> p b m t", m=OBJ).unsqueeze(2).to_broadcast(shape),
                 in1=ab[c][1][:, g, o, :].rearrange("p (b k) t -> p b k t", k=OBJ).unsqueeze(3).to_broadcast(shape),
                 op=ADD,
             )
 
-        def h_relu(u, g):
-            nc.vector.tensor_scalar_max(out=hid[u][1][:, g, :], in0=hid[u][0][:, g, :], scalar1=0.0)
+        def h_relu(x):
+            hid[x].append(ring.tile([P, 2048], BF16, name="h_relu", bufs=2, align_bytes=64))
+            nc.vector.tensor_scalar_max(out=hid[x][1][:], in0=hid[x][0][:], scalar1=0.0)
 
-        def h_quant(u, g):
+        def h_quant(x):
+            u, g = divmod(x, 2)
+            if u not in h_code:
+                h_code[u] = [
+                    ring.tile([P, 2, 512], U32, name="h_code", bufs=3, align_bytes=64),
+                    ring.tile([P, 2, 512], U8, name="h_scale", bufs=3, align_bytes=64),
+                ]
             nc.vector.quantize_mx(
-                out=hid[u][2][:, g, :].bitcast(FP8X4), scales=hid[u][3][:, g, :], in_=hid[u][1][:, g, :]
+                out=h_code[u][0][:, g, :].bitcast(FP8X4), scales=h_code[u][1][:, g, :], in_=hid[x][1][:]
             )
 
         pools = {}
@@ -185,8 +193,8 @@ def tile_pairwiserelationmodule_pa_l_kernel(tc, objs, W1, b1, W2, b2, out_0, out
                     out=y_bank[u, j][:],
                     lhsT=w2_codes[:, g, P * j : P * (j + 1)].bitcast(FP8X4),
                     lhsT_scale=w2_scales[:, g, P * j : P * (j + 1)],
-                    rhs=hid[u][2][:, g, :].bitcast(FP8X4),
-                    rhs_scale=hid[u][3][:, g, :],
+                    rhs=h_code[u][0][:, g, :].bitcast(FP8X4),
+                    rhs_scale=h_code[u][1][:, g, :],
                     start=(g == 0),
                     stop=(g == 1),
                 )
@@ -239,62 +247,64 @@ def tile_pairwiserelationmodule_pa_l_kernel(tc, objs, W1, b1, W2, b2, out_0, out
 
         S_SLOT = {2 * UNITS - 6: (0, 0), 2 * UNITS - 5: (0, 1), 2 * UNITS: (1, 0), 2 * UNITS + 1: (1, 1)}
 
-        def run_slot(slot, early, late_w2):
+        HALVES = 2 * UNITS
+        waiting = {}
+
+        def run_slot(slot):
             u, i = divmod(slot, 2)
             js = list(range(4 * i, 4 * i + 4))
-            tts = (2 * i, 2 * i + 1)
-            add_u, add_g = divmod(slot + 3, 2)
-            fin_u, fin_g = divmod(slot + 2, 2)
-            c1, r1 = divmod(slot + 7, 4)
-            c0 = (slot + 9) // 4 if (slot + 9) % 4 == 0 else CHUNKS
+            x = slot + 4
+            c1, r1 = divmod(slot + 9, 4)
+            c0 = (slot + 11) // 4 if (slot + 11) % 4 == 0 else CHUNKS
+            pu, pi = divmod(slot - 1, 2)
+            if slot - 1 in waiting:
+                stage1_out("v", *waiting[slot - 1])
+            if 1 <= pu <= UNITS:
+                for tt in (2 * pi, 2 * pi + 1):
+                    for hh in range(2):
+                        if (tt, hh) != S_BANK:
+                            x_out("v", pu - 1, tt, hh)
+                    x_store(pu - 1, tt)
             if 0 <= u < UNITS:
                 for j in js[:3]:
                     stage2(u, j)
                 stage2_out(u, js[0])
                 stage2(u, js[3])
-            if slot < 1:
-                sums = early[2 * slot + 2 : 2 * slot + 4]
-            else:
-                sums = [stage1(c1, r1 % 2, r1 // 2, "s1")] if c1 < CHUNKS else []
-            pu, pi = divmod(slot - 1, 2)
-            ptts = (2 * pi, 2 * pi + 1)
-            if 1 <= pu <= UNITS:
-                x_out("v", pu - 1, ptts[0], 0)
-                x_store(pu - 1, ptts[0])
-            if fin_u < UNITS:
-                h_relu(fin_u, fin_g)
-            if 1 <= pu <= UNITS:
-                x_out("v", pu - 1, ptts[1], 0)
-                x_store(pu - 1, ptts[1])
-            if fin_u < UNITS:
-                h_quant(fin_u, fin_g)
-            for g, jq, grouped in late_w2:
-                w2_quant(g, jq, grouped)
+            sums = stage1(c1, r1 % 2, r1 // 2, "s1" if slot >= 2 else "xo") if c1 < CHUNKS else None
             if 1 <= u <= UNITS:
-                for tt in tts:
+                for tt in (2 * i, 2 * i + 1):
                     turn_x(u - 1, tt)
             if 0 <= u < UNITS:
-                for j in js[1:]:
+                for j in js[1:3]:
                     stage2_out(u, j)
-            for done in sums:
-                if done[1] == 0:
-                    stage1_out("s", *done)
-            if add_u < UNITS:
-                h_add(add_u, add_g)
-            for done in sums:
-                if done[1] == 1:
-                    stage1_out("v", *done)
+            if sums is not None:
+                if sums[1] == 0:
+                    stage1_out("s", *sums)
+                else:
+                    waiting[slot] = sums
+            if 0 <= u < UNITS:
+                stage2_out(u, js[3])
+            if 1 <= u <= UNITS and i == 0:
+                x_out("s", u - 1, S_BANK[0], S_BANK[1])
             if c0 < CHUNKS:
                 objs_turn(c0, "s1")
-            s_bank = s_turn(*S_SLOT[slot]) if slot in S_SLOT else None
-            if 1 <= u <= UNITS:
-                for tt in tts:
-                    x_out("s", u - 1, tt, 1)
-            if c0 < CHUNKS:
                 objs_group(c0, "s")
-                objs_quant(c0)
+            s_bank = s_turn(*S_SLOT[slot]) if slot in S_SLOT else None
             if s_bank is not None:
-                s_out("v", S_SLOT[slot][0], S_SLOT[slot][1], s_bank)
+                s_out("s", S_SLOT[slot][0], S_SLOT[slot][1], s_bank)
+            if 4 <= x - 2 < HALVES:
+                h_quant(x - 2)
+            if (slot + 10) % 4 == 0 and 3 <= (slot + 10) // 4 < CHUNKS:
+                objs_quant((slot + 10) // 4)
+            if x < HALVES:
+                h_add(nc.vector, x, g_sets(x), UNIT_SETS)
+            if 4 <= x - 1 < HALVES:
+                h_relu(x - 1)
+            if x + 1 < HALVES:
+                h_add(nc.gpsimd, x + 1, 0, g_sets(x + 1))
+
+        def g_sets(x):
+            return G_SETS if x >= 8 else 0
 
         load_objs(0)
         with tc.tile_pool(name="prep", bufs=2) as prep:
@@ -353,29 +363,46 @@ def tile_pairwiserelationmodule_pa_l_kernel(tc, objs, W1, b1, W2, b2, out_0, out
             stage1_out("s", *sa)
             stage1_out("v", *sb)
             g11 = weights_turn(w1_raw[1, 1], 0)
-            h_add(0, 0)
+            h_add(nc.vector, 0, 0, UNIT_SETS)
             w1_quant(1, 0, g10)
             w1_quant(1, 1, g11)
             g12 = weights_turn(w1_raw[1, 2], 0)
             g13 = weights_turn(w1_raw[1, 3], 0)
-            h_relu(0, 0)
+            h_relu(0)
             w1_quant(1, 2, g12)
             w1_quant(1, 3, g13)
+            g20 = weights_turn(w2_raw[0], 0)
+            g21 = weights_turn(w2_raw[0], 4)
             sa = stage1(0, 0, 1, "s1")
             sb = stage1(0, 1, 1, "y")
             stage1_out("s", *sa)
-            h_quant(0, 0)
+            h_quant(0)
             stage1_out("v", *sb)
-            g20 = weights_turn(w2_raw[0], 0)
             g22 = weights_turn(w2_raw[1], 0)
-            h_add(0, 1)
+            objs_turn(2, "s1")
+            objs_group(2, "s")
+            h_add(nc.vector, 1, 0, UNIT_SETS)
             w2_quant(0, 0, g20)
             w2_quant(1, 0, g22)
-            g21 = weights_turn(w2_raw[0], 4)
             g23 = weights_turn(w2_raw[1], 4)
+            h_relu(1)
+            objs_quant(2)
             early = [stage1(1, r % 2, r // 2, "xo") for r in range(4)]
-            run_slot(-1, early, ((0, 1, g21), (1, 1, g23)))
+            h_quant(1)
+            w2_quant(0, 1, g21)
+            w2_quant(1, 1, g23)
+            stage1_out("s", *early[0])
+            stage1_out("s", *early[2])
+            stage1_out("s", *stage1(2, 0, 0, "s1"))
+            h_add(nc.vector, 2, 0, UNIT_SETS)
+            h_add(nc.vector, 3, 0, UNIT_SETS)
+            h_relu(2)
+            stage1_out("v", *early[1])
+            h_quant(2)
+            h_relu(3)
+            stage1_out("v", *early[3])
+            h_quant(3)
 
         pools["flow"] = ctx.enter_context(tc.tile_pool(name="flow", bufs=2))
         for slot in range(2 * UNITS + 3):
-            run_slot(slot, early, ())
+            run_slot(slot)

@@ -269,8 +269,9 @@ def tile_pairwiserelationmodule_pa_l_kernel(tc, objs, W1, b1, W2, b2, out_0, out
                 for j in js[:3]:
                     stage2(u, j)
                 stage2_out(u, js[0])
-                stage2(u, js[3])
             sums = stage1(c1, r1 % 2, r1 // 2, "s1" if slot >= 2 else "xo") if c1 < CHUNKS else None
+            if 0 <= u < UNITS:
+                stage2(u, js[3])
             if 1 <= u <= UNITS:
                 for tt in (2 * i, 2 * i + 1):
                     turn_x(u - 1, tt)

@@ -19,8 +19,8 @@ P = 128
 UNIT_SETS = 8
 UNITS = SETS // UNIT_SETS
 CHUNKS = SETS * OBJ // P
-S_BANK = (1, 1)
-G_SETS = 3
+S_BANKS = ((1, 1), (3, 1))
+G_SETS = (2, 3)
 BANKS = {"y": 3, "xo": 4, "s1": 1}
 
 
@@ -186,8 +186,8 @@ def tile_pairwiserelationmodule_pa_l_kernel(tc, objs, W1, b1, W2, b2, out_0, out
         x_bank = {}
         x_sb = {}
 
-        def stage2(u, j):
-            y_bank[u, j] = bank("y")
+        def stage2(u, j, tag):
+            y_bank[u, j] = bank(tag)
             for g in range(2):
                 nc.tensor.matmul_mx(
                     out=y_bank[u, j][:],
@@ -234,7 +234,7 @@ def tile_pairwiserelationmodule_pa_l_kernel(tc, objs, W1, b1, W2, b2, out_0, out
 
         def s_turn(h, hh):
             if hh == 0:
-                s_sb[h] = pools["flow"].tile([P, OUTC], F32, name="x_sb", bufs=6)
+                s_sb[h] = pools["flow"].tile([P, OUTC], F32, name="s_sb", bufs=1)
             bk = bank("s1")
             for jj in range(4):
                 nc.tensor.transpose(bk[:, P * jj : P * (jj + 1)], s_t[h][:, 4 * hh + jj, :], ident[:])
@@ -245,7 +245,7 @@ def tile_pairwiserelationmodule_pa_l_kernel(tc, objs, W1, b1, W2, b2, out_0, out
             if hh == 1:
                 nc.sync.dma_start(out=out_1[P * h : P * (h + 1), :], in_=s_sb[h][:])
 
-        S_SLOT = {2 * UNITS - 6: (0, 0), 2 * UNITS - 5: (0, 1), 2 * UNITS: (1, 0), 2 * UNITS + 1: (1, 1)}
+        S_SLOT = {UNITS + 3: (0, 0), UNITS + 7: (0, 1), 2 * UNITS: (1, 0), 2 * UNITS + 1: (1, 1)}
 
         HALVES = 2 * UNITS
         waiting = {}
@@ -262,16 +262,16 @@ def tile_pairwiserelationmodule_pa_l_kernel(tc, objs, W1, b1, W2, b2, out_0, out
             if 1 <= pu <= UNITS:
                 for tt in (2 * pi, 2 * pi + 1):
                     for hh in range(2):
-                        if (tt, hh) != S_BANK:
+                        if (tt, hh) not in s_share(slot - 1):
                             x_out("v", pu - 1, tt, hh)
                     x_store(pu - 1, tt)
             if 0 <= u < UNITS:
                 for j in js[:3]:
-                    stage2(u, j)
+                    stage2(u, j, "y")
                 stage2_out(u, js[0])
             sums = stage1(c1, r1 % 2, r1 // 2, "s1" if slot >= 2 else "xo") if c1 < CHUNKS else None
             if 0 <= u < UNITS:
-                stage2(u, js[3])
+                stage2(u, js[3], "y" if sums is not None else "s1")
             if 1 <= u <= UNITS:
                 for tt in (2 * i, 2 * i + 1):
                     turn_x(u - 1, tt)
@@ -285,8 +285,9 @@ def tile_pairwiserelationmodule_pa_l_kernel(tc, objs, W1, b1, W2, b2, out_0, out
                     waiting[slot] = sums
             if 0 <= u < UNITS:
                 stage2_out(u, js[3])
-            if 1 <= u <= UNITS and i == 0:
-                x_out("s", u - 1, S_BANK[0], S_BANK[1])
+            if 1 <= u <= UNITS:
+                for tt, hh in s_share(slot):
+                    x_out("s", u - 1, tt, hh)
             if c0 < CHUNKS:
                 objs_turn(c0, "s1")
                 objs_group(c0, "s")
@@ -304,8 +305,13 @@ def tile_pairwiserelationmodule_pa_l_kernel(tc, objs, W1, b1, W2, b2, out_0, out
             if x + 1 < HALVES:
                 h_add(nc.gpsimd, x + 1, 0, g_sets(x + 1))
 
+        def s_share(slot):
+            if slot + 5 >= HALVES:
+                return []
+            return [th for th in S_BANKS if th[0] // 2 == slot % 2]
+
         def g_sets(x):
-            return G_SETS if x >= 8 else 0
+            return G_SETS[x % 2] if x >= 8 else 0
 
         load_objs(0)
         with tc.tile_pool(name="prep", bufs=2) as prep:

@@ -20,7 +20,7 @@ UNIT_SETS = 8
 UNITS = SETS // UNIT_SETS
 CHUNKS = SETS * OBJ // P
 S_BANKS = ((1, 1), (3, 1))
-G_SETS = (2, 3)
+G_SETS = (3, 3)
 BANKS = {"y": 3, "xo": 4, "s1": 1}
 
 

from contextlib import ExitStack

import concourse.mybir as mybir
from concourse.masks import make_identity

F32 = mybir.dt.float32
BF16 = mybir.dt.bfloat16
U32 = mybir.dt.uint32
U8 = mybir.dt.uint8
FP8X4 = mybir.dt.float8_e4m3fn_x4
RELU = mybir.ActivationFunctionType.Relu
ADD = mybir.AluOpType.add

SETS, OBJ, FEAT, HID, OUTC = 256, 8, 1024, 1024, 1024
PAIRS = OBJ * OBJ
FLOPS = 2 * SETS * PAIRS * (2 * FEAT * HID + HID * OUTC)

P = 128
UNIT_SETS = 8
UNITS = SETS // UNIT_SETS
CHUNKS = SETS * OBJ // P
S_BANKS = ((1, 1), (3, 1))
G_SETS = (3, 3)
BANKS = {"y": 3, "xo": 4, "s1": 1}


def tile_pairwiserelationmodule_pa_l_kernel(tc, objs, W1, b1, W2, b2, out_0, out_1):
    nc = tc.nc
    objs_rows = objs.flatten_outer_dims()
    x_rows = out_0.flatten_outer_dims()

    with ExitStack() as ctx:
        ctx.enter_context(tc.manual_schedule())
        keep = ctx.enter_context(tc.tile_pool(name="keep", bufs=1))
        ring = ctx.enter_context(tc.tile_pool(name="ring", bufs=2))
        psum = ctx.enter_context(tc.psum_pool(name="psum", bufs=2))

        def bank(tag):
            return psum.tile([P, 512], F32, name="bank_" + tag, tag=tag, bufs=BANKS[tag])

        ident = keep.tile([P, P], F32, name="ident")
        make_identity(nc, ident[:])
        b1_bf = keep.tile([P, 2, 4], BF16, name="b1_bf")
        b2_bf = keep.tile([P, 8], BF16, name="b2_bf")
        b1_f = keep.tile([P, 2, 4], F32, name="b1_f")
        b2_f = keep.tile([P, 8], F32, name="b2_f")
        warm = keep.tile([P, 1], F32, name="warm")
        w1_codes = keep.tile([P, 4, HID], U32, name="w1_codes", align_bytes=64)
        w1_scales = keep.tile([P, 4, HID], U8, name="w1_scales", align_bytes=64)
        w2_codes = keep.tile([P, 2, OUTC], U32, name="w2_codes", align_bytes=64)
        w2_scales = keep.tile([P, 2, OUTC], U8, name="w2_scales", align_bytes=64)
        s_t = [keep.tile([P, 8, P], F32, name="s_t%d" % h) for h in range(2)]
        obj_raw = [keep.tile([P, 2, FEAT], BF16, name="obj_raw%d" % r) for r in range(8)]

        with nc.allow_non_contiguous_dma(reason="two small bias vectors, one or four elements a partition"):
            nc.scalar.dma_start(out=b1_bf[:], in_=b1.rearrange("(g p t) -> p g t", g=2, t=4))
            nc.scalar.dma_start(out=b2_bf[:], in_=b2.rearrange("(j p) -> p j", p=P))
        nc.vector.memset(warm[:], 0.0)
        nc.scalar.activation(out=warm[:], in_=warm[:], func=RELU)

        def load_objs(r):
            nc.sync.dma_start(
                out=obj_raw[r][:],
                in_=objs_rows[256 * r : 256 * (r + 1), :].rearrange("(i p) k -> p i k", p=P),
            )

        def copy_out(engine, out, in_):
            if engine == "v":
                nc.vector.tensor_copy(out=out, in_=in_)
            else:
                nc.scalar.copy(out=out, in_=in_)

        def turn_two(tag, rows_a, rows_b):
            bk = bank(tag)
            view = bk[:].rearrange("p (s u r) -> p s u r", s=2, u=2)
            for s, rows in enumerate((rows_a, rows_b)):
                words = rows.bitcast(F32)
                for u in range(2):
                    nc.tensor.transpose(view[:, s, u, :], words[:, u : 256 : 2], ident[:])
            return view.rearrange("p s u r -> p s r u")

        def group_two(engine, turned, grouped_words):
            copy_out(engine, grouped_words.rearrange("p (s r u) -> p s r u", s=2, u=2), turned)

        obj_q = {}
        ab = {}

        def objs_turn(c, tag):
            rows = obj_raw[c // 2][:, c % 2, :]
            obj_q[c] = [
                turn_two(tag, rows[:, 0:512], rows[:, 512:1024]),
                ring.tile([P, 1024], BF16, name="obj_grouped", bufs=2, align_bytes=64),
                ring.tile([P, 2, P], U32, name="obj_code", bufs=4, align_bytes=64),
                ring.tile([P, 2, P], U8, name="obj_scale", bufs=4, align_bytes=64),
            ]

        def objs_group(c, engine):
            group_two(engine, obj_q[c][0], obj_q[c][1][:].bitcast(F32))

        def objs_quant(c):
            nc.vector.quantize_mx(
                out=obj_q[c][2][:].rearrange("p c o -> p (c o)").bitcast(FP8X4),
                scales=obj_q[c][3][:].rearrange("p c o -> p (c o)"),
                in_=obj_q[c][1][:],
            )

        def stage1(c, half, g, tag):
            if c not in ab:
                ab[c] = [
                    ring.tile([P, 2, P, 4], F32, name="a_sum", bufs=3),
                    ring.tile([P, 2, P, 4], F32, name="b_sum", bufs=3),
                ]
            codes, scales = obj_q[c][2], obj_q[c][3]
            bk = bank(tag)
            view = bk[:].rearrange("p (t o) -> p t o", t=4)
            for t in range(4):
                cols = slice(512 * g + P * t, 512 * g + P * (t + 1))
                for c2 in range(2):
                    nc.tensor.matmul_mx(
                        out=view[:, t, :],
                        lhsT=w1_codes[:, 2 * half + c2, cols].bitcast(FP8X4),
                        lhsT_scale=w1_scales[:, 2 * half + c2, cols],
                        rhs=codes[:, c2, :].bitcast(FP8X4),
                        rhs_scale=scales[:, c2, :],
                        start=(c2 == 0),
                        stop=(c2 == 1),
                    )
            return (c, half, g, view.rearrange("p t o -> p o t"))

        def stage1_out(engine, c, half, g, sums):
            if half == 0:
                copy_out(engine, ab[c][0][:, g, :, :], sums)
            else:
                nc.vector.tensor_tensor(
                    out=ab[c][1][:, g, :, :],
                    in0=sums,
                    in1=b1_f[:, g, :].unsqueeze(1).to_broadcast([P, P, 4]),
                    op=ADD,
                )

        hid = {}
        h_code = {}

        def h_add(engine, x, b0, b_end):
            u, g = divmod(x, 2)
            if x not in hid:
                hid[x] = [ring.tile([P, 2048], BF16, name="h_sum", bufs=2, align_bytes=64)]
            if b_end == b0:
                return
            c, hf = divmod(u, 2)
            o = slice(64 * hf + OBJ * b0, 64 * hf + OBJ * b_end)
            shape = [P, b_end - b0, OBJ, OBJ, 4]
            engine.tensor_tensor(
                out=hid[x][0][:, 256 * b0 : 256 * b_end].rearrange("p (b k m t) -> p b k m t", k=OBJ, m=OBJ, t=4),
                in0=ab[c][0][:, g, o, :].rearrange("p (b m) t -> p b m t", m=OBJ).unsqueeze(2).to_broadcast(shape),
                in1=ab[c][1][:, g, o, :].rearrange("p (b k) t -> p b k t", k=OBJ).unsqueeze(3).to_broadcast(shape),
                op=ADD,
            )

        def h_relu(x):
            hid[x].append(ring.tile([P, 2048], BF16, name="h_relu", bufs=2, align_bytes=64))
            nc.vector.tensor_scalar_max(out=hid[x][1][:], in0=hid[x][0][:], scalar1=0.0)

        def h_quant(x):
            u, g = divmod(x, 2)
            if u not in h_code:
                h_code[u] = [
                    ring.tile([P, 2, 512], U32, name="h_code", bufs=3, align_bytes=64),
                    ring.tile([P, 2, 512], U8, name="h_scale", bufs=3, align_bytes=64),
                ]
            nc.vector.quantize_mx(
                out=h_code[u][0][:, g, :].bitcast(FP8X4), scales=h_code[u][1][:, g, :], in_=hid[x][1][:]
            )

        pools = {}

        def w2_quant(g, jq, grouped):
            nc.vector.quantize_mx(
                out=w2_codes[:, g, 512 * jq : 512 * (jq + 1)].bitcast(FP8X4),
                scales=w2_scales[:, g, 512 * jq : 512 * (jq + 1)],
                in_=grouped[:],
            )

        y_bank = {}
        x_t = {}
        x_bank = {}
        x_sb = {}

        def stage2(u, j, tag):
            y_bank[u, j] = bank(tag)
            for g in range(2):
                nc.tensor.matmul_mx(
                    out=y_bank[u, j][:],
                    lhsT=w2_codes[:, g, P * j : P * (j + 1)].bitcast(FP8X4),
                    lhsT_scale=w2_scales[:, g, P * j : P * (j + 1)],
                    rhs=h_code[u][0][:, g, :].bitcast(FP8X4),
                    rhs_scale=h_code[u][1][:, g, :],
                    start=(g == 0),
                    stop=(g == 1),
                )

        def stage2_out(u, j):
            x_t[u, j] = pools["flow"].tile([P, 512], F32, name="x_t", bufs=16)
            for bl in range(UNIT_SETS):
                b = UNIT_SETS * u + bl
                nc.scalar.activation(
                    out=x_t[u, j][:, PAIRS * bl : PAIRS * (bl + 1)],
                    in_=y_bank[u, j][:, PAIRS * bl : PAIRS * (bl + 1)],
                    func=RELU,
                    bias=b2_f[:, j : j + 1],
                    scale=1.0,
                    accum_out=s_t[b // P][:, j, b % P : b % P + 1],
                )

        def turn_x(u, tt):
            x_sb[u, tt] = pools["flow"].tile([P, OUTC], F32, name="x_sb", bufs=6)
            for hh in range(2):
                x_bank[u, tt, hh] = bank("xo")
                for jj in range(4):
                    nc.tensor.transpose(
                        x_bank[u, tt, hh][:, P * jj : P * (jj + 1)],
                        x_t[u, 4 * hh + jj][:, P * tt : P * (tt + 1)],
                        ident[:],
                    )

        def x_out(engine, u, tt, hh):
            copy_out(engine, x_sb[u, tt][:, 512 * hh : 512 * (hh + 1)], x_bank[u, tt, hh][:])

        def x_store(u, tt):
            r0 = 512 * u + P * tt
            nc.sync.dma_start(out=x_rows[r0 : r0 + P, :], in_=x_sb[u, tt][:])

        s_sb = {}

        def s_turn(h, hh):
            if hh == 0:
                s_sb[h] = pools["flow"].tile([P, OUTC], F32, name="s_sb", bufs=1)
            bk = bank("s1")
            for jj in range(4):
                nc.tensor.transpose(bk[:, P * jj : P * (jj + 1)], s_t[h][:, 4 * hh + jj, :], ident[:])
            return bk

        def s_out(engine, h, hh, bk):
            copy_out(engine, s_sb[h][:, 512 * hh : 512 * (hh + 1)], bk[:])
            if hh == 1:
                nc.sync.dma_start(out=out_1[P * h : P * (h + 1), :], in_=s_sb[h][:])

        S_SLOT = {UNITS + 3: (0, 0), UNITS + 7: (0, 1), 2 * UNITS: (1, 0), 2 * UNITS + 1: (1, 1)}

        HALVES = 2 * UNITS
        waiting = {}

        def run_slot(slot):
            u, i = divmod(slot, 2)
            js = list(range(4 * i, 4 * i + 4))
            x = slot + 4
            c1, r1 = divmod(slot + 9, 4)
            c0 = (slot + 11) // 4 if (slot + 11) % 4 == 0 else CHUNKS
            pu, pi = divmod(slot - 1, 2)
            if slot - 1 in waiting:
                stage1_out("v", *waiting[slot - 1])
            if 1 <= pu <= UNITS:
                for tt in (2 * pi, 2 * pi + 1):
                    for hh in range(2):
                        if (tt, hh) not in s_share(slot - 1):
                            x_out("v", pu - 1, tt, hh)
                    x_store(pu - 1, tt)
            if 0 <= u < UNITS:
                for j in js[:3]:
                    stage2(u, j, "y")
                stage2_out(u, js[0])
            sums = stage1(c1, r1 % 2, r1 // 2, "s1" if slot >= 2 else "xo") if c1 < CHUNKS else None
            if 0 <= u < UNITS:
                stage2(u, js[3], "y" if sums is not None else "s1")
            if 1 <= u <= UNITS:
                for tt in (2 * i, 2 * i + 1):
                    turn_x(u - 1, tt)
            if 0 <= u < UNITS:
                for j in js[1:3]:
                    stage2_out(u, j)
            if sums is not None:
                if sums[1] == 0:
                    stage1_out("s", *sums)
                else:
                    waiting[slot] = sums
            if 0 <= u < UNITS:
                stage2_out(u, js[3])
            if 1 <= u <= UNITS:
                for tt, hh in s_share(slot):
                    x_out("s", u - 1, tt, hh)
            if c0 < CHUNKS:
                objs_turn(c0, "s1")
                objs_group(c0, "s")
            s_bank = s_turn(*S_SLOT[slot]) if slot in S_SLOT else None
            if s_bank is not None:
                s_out("s", S_SLOT[slot][0], S_SLOT[slot][1], s_bank)
            if 4 <= x - 2 < HALVES:
                h_quant(x - 2)
            if (slot + 10) % 4 == 0 and 3 <= (slot + 10) // 4 < CHUNKS:
                objs_quant((slot + 10) // 4)
            if x < HALVES:
                h_add(nc.vector, x, g_sets(x), UNIT_SETS)
            if 4 <= x - 1 < HALVES:
                h_relu(x - 1)
            if x + 1 < HALVES:
                h_add(nc.gpsimd, x + 1, 0, g_sets(x + 1))

        def s_share(slot):
            if slot + 5 >= HALVES:
                return []
            return [th for th in S_BANKS if th[0] // 2 == slot % 2]

        def g_sets(x):
            return G_SETS[x % 2] if x >= 8 else 0

        load_objs(0)
        with tc.tile_pool(name="prep", bufs=2) as prep:
            w1_raw = {}
            for g in range(2):
                for q in range(4):
                    w1_raw[g, q] = prep.tile([P, 4, 512], BF16, name="w1_raw", bufs=8)
                    nc.sync.dma_start(
                        out=w1_raw[g, q][:],
                        in_=W1[512 * g : 512 * (g + 1), 512 * q : 512 * (q + 1)].rearrange("(m t) k -> m t k", t=4),
                    )
            w2_raw = {}
            for g in range(2):
                w2_raw[g] = prep.tile([P, 8, 512], BF16, name="w2_raw", bufs=2)
                nc.sync.dma_start(
                    out=w2_raw[g][:],
                    in_=W2[:, 512 * g : 512 * (g + 1)].rearrange("(j p) k -> p j k", p=P),
                )
            for r in range(1, 8):
                load_objs(r)

            nc.vector.tensor_copy(out=b1_f[:], in_=b1_bf[:])
            nc.vector.tensor_copy(out=b2_f[:], in_=b2_bf[:])

            spare = ["xo", "y", "xo", "y", "xo", "y", "xo"]
            count = [0]

            def weights_turn(raw, slot0):
                grouped = prep.tile([P, 2048], BF16, name="w_grouped", bufs=4, align_bytes=64)
                words = grouped[:].bitcast(F32)
                for d in (0, 2):
                    tag = spare[count[0] % 7]
                    count[0] += 1
                    turned = turn_two(tag, raw[:, slot0 + d, :], raw[:, slot0 + d + 1, :])
                    group_two("s", turned, words[:, 256 * d : 256 * d + 512])
                return grouped

            def w1_quant(g, q, grouped):
                nc.vector.quantize_mx(
                    out=w1_codes[:, q, 512 * g : 512 * (g + 1)].bitcast(FP8X4),
                    scales=w1_scales[:, q, 512 * g : 512 * (g + 1)],
                    in_=grouped[:],
                )

            objs_turn(0, "s1")
            objs_turn(1, "y")
            objs_group(0, "s")
            objs_group(1, "s")
            objs_quant(0)
            objs_quant(1)
            for q in range(4):
                w1_quant(0, q, weights_turn(w1_raw[0, q], 0))
            g10 = weights_turn(w1_raw[1, 0], 0)
            sa = stage1(0, 0, 0, "s1")
            sb = stage1(0, 1, 0, "y")
            stage1_out("s", *sa)
            stage1_out("v", *sb)
            g11 = weights_turn(w1_raw[1, 1], 0)
            h_add(nc.vector, 0, 0, UNIT_SETS)
            w1_quant(1, 0, g10)
            w1_quant(1, 1, g11)
            g12 = weights_turn(w1_raw[1, 2], 0)
            g13 = weights_turn(w1_raw[1, 3], 0)
            h_relu(0)
            w1_quant(1, 2, g12)
            w1_quant(1, 3, g13)
            g20 = weights_turn(w2_raw[0], 0)
            g21 = weights_turn(w2_raw[0], 4)
            sa = stage1(0, 0, 1, "s1")
            sb = stage1(0, 1, 1, "y")
            stage1_out("s", *sa)
            h_quant(0)
            stage1_out("v", *sb)
            g22 = weights_turn(w2_raw[1], 0)
            objs_turn(2, "s1")
            objs_group(2, "s")
            h_add(nc.vector, 1, 0, UNIT_SETS)
            w2_quant(0, 0, g20)
            w2_quant(1, 0, g22)
            g23 = weights_turn(w2_raw[1], 4)
            h_relu(1)
            objs_quant(2)
            early = [stage1(1, r % 2, r // 2, "xo") for r in range(4)]
            h_quant(1)
            w2_quant(0, 1, g21)
            w2_quant(1, 1, g23)
            stage1_out("s", *early[0])
            stage1_out("s", *early[2])
            stage1_out("s", *stage1(2, 0, 0, "s1"))
            h_add(nc.vector, 2, 0, UNIT_SETS)
            h_add(nc.vector, 3, 0, UNIT_SETS)
            h_relu(2)
            stage1_out("v", *early[1])
            h_quant(2)
            h_relu(3)
            stage1_out("v", *early[3])
            h_quant(3)

        pools["flow"] = ctx.enter_context(tc.tile_pool(name="flow", bufs=2))
        for slot in range(2 * UNITS + 3):
            run_slot(slot)
